import numpy as np
import ml_dtypes


def mxq(x, axis, fmt="e4m3"):
    dtype, down = {"e4m3": (ml_dtypes.float8_e4m3fn, 7), "e5m2": (ml_dtypes.float8_e5m2, 14)}[fmt]
    v = np.moveaxis(np.asarray(x, np.float32).astype(ml_dtypes.bfloat16).astype(np.float64), axis, -1)
    blocks = v.reshape(v.shape[:-1] + (-1, 32))
    amax = np.abs(blocks).max(-1, keepdims=True)
    byte = np.maximum(np.where(amax > 0, np.frexp(amax)[1] - 1 + 127, 0) - down, 1)
    scale = np.exp2(byte - 127.0)
    codes = (blocks / scale).astype(np.float32).astype(dtype).astype(np.float64)
    return np.moveaxis((codes * scale).reshape(v.shape), -1, axis)


WIDE = False


def mx_kscale(k):
    if not WIDE:
        return np.ones(k)
    levels = np.array([10, -10, 5, -5, 0])
    if k % 512:
        return np.exp2(np.random.permutation(np.resize(levels, k // 32))).repeat(32)
    a = np.empty((k // 512, 16))
    for p in range(k // 512):
        a[p, :8] = np.random.permutation(np.resize(levels, 8))
        for g in range(8):
            far = levels[np.abs(levels - a[p, g]) >= 10]
            a[p, g + 8] = far[np.random.randint(len(far))]
    return np.exp2(a.ravel()).repeat(32)


BF16 = ml_dtypes.bfloat16


def bf(x):
    return np.asarray(x, np.float32).astype(BF16)


def f64(x):
    return np.asarray(x).astype(np.float64)


B, S, D, E = 2, 512, 512, 512
SC = 1.5


def draw0():
    s, t = mx_kscale(D), mx_kscale(E)
    rn = np.random.standard_normal
    qs = np.sqrt(SC / np.sqrt(2.0 * E))
    ws = qs / np.sqrt(2.0 * D)
    return {"x_re": bf(rn((B, S, D)) * s), "x_im": bf(rn((B, S, D)) * s),
            "Wq_re": bf(rn((E, D)) * ws * t[:, None] / s), "Wq_im": bf(rn((E, D)) * ws * t[:, None] / s),
            "bq_re": bf(rn(E) * 0.5 * qs * t), "bq_im": bf(rn(E) * 0.5 * qs * t),
            "Wk_re": bf(rn((E, D)) * ws / t[:, None] / s), "Wk_im": bf(rn((E, D)) * ws / t[:, None] / s),
            "bk_re": bf(rn(E) * 0.5 * qs / t), "bk_im": bf(rn(E) * 0.5 * qs / t)}


def cproj(xr, xi, w_re, w_im, b_re, b_im):
    wr = mxq(f64(w_re), 1, "e4m3").T
    wi = mxq(f64(w_im), 1, "e4m3").T
    y_re = (xr @ wr) - (xi @ wi) + f64(b_re)
    y_im = (xr @ wi) + (xi @ wr) + f64(b_im)
    return y_re, y_im


def core(x_re, x_im, Wq_re, Wq_im, bq_re, bq_im, Wk_re, Wk_im, bk_re, bk_im):
    xr = mxq(f64(x_re), 2, "e4m3")
    xi = mxq(f64(x_im), 2, "e4m3")
    q_re, q_im = cproj(xr, xi, Wq_re, Wq_im, bq_re, bq_im)
    k_re, k_im = cproj(xr, xi, Wk_re, Wk_im, bk_re, bk_im)
    return ((mxq(q_re, 2, "e4m3") @ mxq(k_re, 2, "e4m3").transpose(0, 2, 1))
            + (mxq(q_im, 2, "e4m3") @ mxq(k_im, 2, "e4m3").transpose(0, 2, 1)))


def e4m3fn_bytes(y):
    return np.clip(np.asarray(y, np.float64), -448.0, 448.0).astype(np.float32).astype(ml_dtypes.float8_e4m3fn).view(np.uint8)


def e4m3fn_values(b):
    return np.asarray(b, np.uint8).view(ml_dtypes.float8_e4m3fn).astype(np.float64)


def setup_inputs():
    d = draw0()
    x0 = np.asarray(d['x_re']).astype(np.float64)
    s = (np.max(np.abs(x0), axis=(0, 1), keepdims=True) / 448.0).astype(np.float32)
    out = {}
    for k, v in d.items():
        if k == 'x_re':
            out['x_re_bytes'] = e4m3fn_bytes(x0 / s.astype(np.float64))
            out['x_re_scale'] = s
        else:
            out[k] = v
    return out


def reference(x_re_bytes, x_re_scale, x_im, Wq_re, Wq_im, bq_re, bq_im, Wk_re, Wk_im, bk_re, bk_im):
    return core(e4m3fn_values(x_re_bytes) * x_re_scale.astype(np.float64), x_im, Wq_re, Wq_im, bq_re, bq_im, Wk_re, Wk_im, bk_re, bk_im)

@@ -1,0 +1,241 @@
+from contextlib import ExitStack
+
+import concourse.mybir as mybir
+from concourse.masks import make_identity
+
+FLOPS = 8 * 2 * 1024 * 512 * 512 + 2 * 2 * 2 * 512 * 512 * 512
+
+F32 = mybir.dt.float32
+BF16 = mybir.dt.bfloat16
+U32 = mybir.dt.uint32
+U8 = mybir.dt.uint8
+FP8 = mybir.dt.float8_e4m3fn
+FP8X4 = mybir.dt.float8_e4m3fn_x4
+ALU = mybir.AluOpType
+ACT = mybir.ActivationFunctionType
+
+P = 128
+K = 512
+BATCHES = 2
+
+
+def tile_teleportationattention_pa_kernel(
+    tc, x_re_bytes, x_re_scale, x_im, Wq_re, Wq_im, bq_re, bq_im, Wk_re, Wk_im, bk_re, bk_im, out
+):
+    nc = tc.nc
+    with ExitStack() as ctx:
+        keep = ctx.enter_context(tc.tile_pool(name="keep", bufs=1))
+        psum = ctx.enter_context(tc.psum_pool(name="psum", bufs=8))
+
+        def new(name, shape, dtype):
+            return keep.tile(shape, dtype, name=name, align_bytes=64)
+
+        def bank_tile():
+            return psum.tile([P, 512], F32, name="bank")
+
+        ident = new("ident", [P, P], F32)
+        warm = new("warm", [P, 1], F32)
+        scale_col = new("scale_col", [P, 4], F32)
+        scale_row = new("scale_row", [P, K], F32)
+        bias_in = {"qr": bq_re, "qi": bq_im, "kr": bk_re, "ki": bk_im}
+        bias = {}
+        for n in bias_in:
+            bias[n] = new("bias_" + n, [P, 4], BF16)
+
+        raw = {}
+        for n in ("wqr", "wqi", "wkr", "wki", "xr0", "xi0", "xr1", "xi1"):
+            raw[n] = new("raw_" + n, [P, 4, K], BF16)
+        xbytes = [new("xbytes%d" % b, [P, 4, K], U8) for b in range(BATCHES)]
+        grouped = {}
+        codes = {}
+        scales = {}
+        for n in ("wqr", "wqi", "wkr", "wki", "xr0", "xi0", "xn0", "xr1", "xi1", "xn1", "qr0", "qi0", "kr0", "ki0", "qr1", "qi1", "kr1", "ki1"):
+            grouped[n] = new("grp_" + n, [P, 4 * 512], BF16)
+            codes[n] = new("codes_" + n, [P, 512], U32)
+            scales[n] = new("scales_" + n, [P, 512], U8)
+        planes = {}
+        for n in ("qr0", "qi0", "kr0", "ki0", "qr1", "qi1", "kr1", "ki1"):
+            planes[n] = new("planes_" + n, [P, 4, 512], BF16)
+        result = [new("result%d" % b, [P, 4, 512], F32) for b in range(BATCHES)]
+
+        w_view = {"wqr": Wq_re, "wqi": Wq_im, "wkr": Wk_re, "wki": Wk_im}
+        src = {}
+        for n in w_view:
+            src[n] = w_view[n].rearrange("(m s) k -> m s k", s=4)
+        for b in range(BATCHES):
+            src["xi%d" % b] = x_im[b].rearrange("(m s) k -> m s k", s=4)
+
+        def load(n, parts=1):
+            step = 4 // parts
+            for i in range(parts):
+                nc.sync.dma_start(out=raw[n][:, i * step : (i + 1) * step, :], in_=src[n][:, i * step : (i + 1) * step, :])
+
+        def load_bytes(b):
+            nc.sync.dma_start(out=xbytes[b][:], in_=x_re_bytes[b].rearrange("(m s) k -> m s k", s=4))
+
+        def widen(b, s):
+            nc.vector.tensor_tensor(
+                out=raw["xr%d" % b][:, s, :], in0=xbytes[b][:, s, :].bitcast(FP8), in1=scale_row[:], op=ALU.mult
+            )
+
+        def turn(n):
+            for h in range(2):
+                bank = bank_tile()
+                v = bank[:].rearrange("p (c u r) -> p c u r", c=2, u=2)
+                for c in range(2):
+                    words = raw[n][:, 2 * h + c, :].bitcast(F32)
+                    for u in range(2):
+                        nc.tensor.transpose(v[:, c, u, :], words[:, u:256:2], ident[:])
+                nc.scalar.copy(
+                    out=grouped[n][:, 1024 * h : 1024 * (h + 1)].bitcast(F32).rearrange("p (c r u) -> p c r u", c=2, u=2),
+                    in_=v.rearrange("p c u r -> p c r u"),
+                )
+
+        def quant(n, h=None):
+            lo, hi = (0, 512) if h is None else (256 * h, 256 * (h + 1))
+            nc.vector.quantize_mx(
+                out=codes[n][:, lo:hi].bitcast(FP8X4), scales=scales[n][:, lo:hi], in_=grouped[n][:, 4 * lo : 4 * hi]
+            )
+
+        def negate(b):
+            nc.vector.tensor_scalar(out=grouped["xn%d" % b][:], in0=grouped["xi%d" % b][:], scalar1=-1.0, scalar2=None, op0=ALU.mult)
+
+        def mm(bank, w, t, x, start, stop):
+            nc.tensor.matmul_mx(
+                out=bank[:],
+                lhsT=codes[w][:, 128 * t : 128 * (t + 1)].bitcast(FP8X4),
+                lhsT_scale=scales[w][:, 128 * t : 128 * (t + 1)],
+                rhs=codes[x][:].bitcast(FP8X4),
+                rhs_scale=scales[x][:],
+                start=start,
+                stop=stop,
+            )
+
+        def operands(side, part, b):
+            if part == "r":
+                return [("w%sr" % side, "xr%d" % b), ("w%si" % side, "xn%d" % b)]
+            return [("w%sr" % side, "xi%d" % b), ("w%si" % side, "xr%d" % b)]
+
+        def leave(bank, side, part, b, t, engine):
+            plane = planes["%s%s%d" % (side, part, b)][:, t, :]
+            column = bias[side + part][:, t : t + 1]
+            if engine == "scalar":
+                nc.scalar.activation(out=plane, in_=bank[:], func=ACT.Identity, bias=column, scale=1.0)
+            else:
+                nc.vector.tensor_scalar(out=plane, in0=bank[:], scalar1=column, scalar2=None, op0=ALU.add)
+
+        def unit(side, part, b, on_vector=()):
+            ops = operands(side, part, b)
+            for t in range(4):
+                bank = bank_tile()
+                for i in range(2):
+                    mm(bank, ops[i][0], t, ops[i][1], i == 0, i == 1)
+                leave(bank, side, part, b, t, "vector" if t in on_vector else "scalar")
+
+        def interleave(n, h):
+            nc.vector.tensor_copy(
+                out=grouped[n][:, 1024 * h : 1024 * (h + 1)].rearrange("p (n t) -> p n t", t=4),
+                in_=planes[n][:, :, 256 * h : 256 * (h + 1)].rearrange("p t n -> p n t"),
+            )
+
+        def pack(n):
+            interleave(n, 0)
+            interleave(n, 1)
+            quant(n, 0)
+            quant(n, 1)
+
+        def score_pass(bank, b, s, part, start, stop):
+            q = "q%s%d" % (part, b)
+            k = "k%s%d" % (part, b)
+            nc.tensor.matmul_mx(
+                out=bank[:],
+                lhsT=codes[q][:, 128 * s : 128 * (s + 1)].bitcast(FP8X4),
+                lhsT_scale=scales[q][:, 128 * s : 128 * (s + 1)],
+                rhs=codes[k][:].bitcast(FP8X4),
+                rhs_scale=scales[k][:],
+                start=start,
+                stop=stop,
+            )
+
+        def score_out(bank, b, s, engine):
+            o = result[b][:, s, :].rearrange("p (m j) -> p m j", j=4)
+            i = bank[:].rearrange("p (j m) -> p m j", j=4)
+            if engine == "scalar":
+                nc.scalar.copy(out=o, in_=i)
+            else:
+                nc.vector.tensor_copy(out=o, in_=i)
+            nc.sync.dma_start(out=out[b].rearrange("(m s) k -> m s k", s=4)[:, s, :], in_=result[b][:, s, :])
+
+        with tc.manual_schedule():
+            nc.scalar.dma_start(out=scale_col[:], in_=x_re_scale.rearrange("a b (p j) -> (a b p) j", j=4))
+            load_bytes(0)
+            load("xi0", 2)
+            load("wqr", 2)
+            load("wqi")
+            load_bytes(1)
+            load("wkr")
+            load("wki")
+            for n in bias_in:
+                nc.sync.dma_start(out=bias[n][:], in_=bias_in[n].rearrange("(p t) -> p t", t=4))
+            load("xi1")
+
+            make_identity(nc, ident[:])
+            nc.vector.memset(warm[:], 0.0)
+            nc.scalar.activation(out=warm[:], in_=warm[:], func=ACT.Identity, bias=0.0, scale=1.0)
+
+            bank = bank_tile()
+            for j in range(4):
+                nc.tensor.transpose(bank[:, 128 * j : 128 * (j + 1)], scale_col[:, j : j + 1].to_broadcast([P, P]), ident[:])
+            nc.scalar.copy(out=scale_row[:].rearrange("p (n j) -> p n j", j=4), in_=bank[:].rearrange("p (j n) -> p n j", j=4))
+
+            turn("xi0")
+            for s in range(4):
+                widen(0, s)
+            turn("wqr")
+            negate(0)
+            quant("xi0")
+            turn("xr0")
+            widen(1, 0)
+            widen(1, 1)
+            quant("wqr")
+            quant("xr0")
+            turn("wqi")
+            widen(1, 2)
+            widen(1, 3)
+            turn("wkr")
+            turn("wki")
+            quant("wqi")
+            quant("wkr")
+            quant("wki")
+            turn("xr1")
+            turn("xi1")
+            quant("xr1")
+            quant("xi1")
+            negate(1)
+            unit("q", "i", 0, (3,))
+            quant("xn0")
+            unit("k", "i", 0)
+            pack("qi0")
+            pack("ki0")
+            unit("q", "i", 1, (3,))
+            quant("xn1")
+            unit("k", "i", 1)
+            pack("qi1")
+            unit("q", "r", 0)
+            pack("ki1")
+            unit("k", "r", 0)
+            pack("qr0")
+            unit("q", "r", 1)
+            pack("kr0")
+            unit("k", "r", 1)
+            pack("qr1")
+            banks = {}
+            for b in range(BATCHES):
+                for s in range(4):
+                    banks[b, s] = bank_tile()
+                    score_pass(banks[b, s], b, s, "i", True, False)
+            pack("kr1")
+            for b in range(BATCHES):
+                for s in range(4):
+                    score_pass(banks[b, s], b, s, "r", False, True)
+                    score_out(banks[b, s], b, s, "vector" if (b, s) in ((0, 2), (1, 1), (1, 3)) else "scalar")

@@ -34,7 +34,8 @@ def tile_teleportationattention_pa_kernel(
             return psum.tile([P, 512], F32, name="bank")
 
         ident = new("ident", [P, P], F32)
-        warm = new("warm", [P, 1], F32)
+        warm = new("warm", [P, 512], BF16)
+        dummy = new("dummy", [P, 1], F32)
         scale_col = new("scale_col", [P, 4], F32)
         scale_row = new("scale_row", [P, K], F32)
         bias_in = {"qr": bq_re, "qi": bq_im, "kr": bk_re, "ki": bk_im}
@@ -78,7 +79,7 @@ def tile_teleportationattention_pa_kernel(
                 out=raw["xr%d" % b][:, s, :], in0=xbytes[b][:, s, :].bitcast(FP8), in1=scale_row[:], op=ALU.mult
             )
 
-        def turn(n):
+        def turn(n, on_vector=()):
             for h in range(2):
                 bank = bank_tile()
                 v = bank[:].rearrange("p (c u r) -> p c u r", c=2, u=2)
@@ -86,10 +87,11 @@ def tile_teleportationattention_pa_kernel(
                     words = raw[n][:, 2 * h + c, :].bitcast(F32)
                     for u in range(2):
                         nc.tensor.transpose(v[:, c, u, :], words[:, u:256:2], ident[:])
-                nc.scalar.copy(
-                    out=grouped[n][:, 1024 * h : 1024 * (h + 1)].bitcast(F32).rearrange("p (c r u) -> p c r u", c=2, u=2),
-                    in_=v.rearrange("p c u r -> p c r u"),
-                )
+                target = grouped[n][:, 1024 * h : 1024 * (h + 1)].bitcast(F32).rearrange("p (c r u) -> p c r u", c=2, u=2)
+                if h in on_vector:
+                    nc.vector.tensor_copy(out=target, in_=v.rearrange("p c u r -> p c r u"))
+                else:
+                    nc.scalar.copy(out=target, in_=v.rearrange("p c u r -> p c r u"))
 
         def quant(n, h=None):
             lo, hi = (0, 512) if h is None else (256 * h, 256 * (h + 1))
@@ -134,8 +136,8 @@ def tile_teleportationattention_pa_kernel(
 
         def interleave(n, h):
             nc.vector.tensor_copy(
-                out=grouped[n][:, 1024 * h : 1024 * (h + 1)].rearrange("p (n t) -> p n t", t=4),
-                in_=planes[n][:, :, 256 * h : 256 * (h + 1)].rearrange("p t n -> p n t"),
+                out=grouped[n][:, 1024 * h : 1024 * (h + 1)].rearrange("p (c i t) -> p c t i", i=4, t=4),
+                in_=planes[n][:, :, 256 * h : 256 * (h + 1)].rearrange("p t (c i) -> p c t i", i=4),
             )
 
         def pack(n):
@@ -168,27 +170,31 @@ def tile_teleportationattention_pa_kernel(
 
         with tc.manual_schedule():
             nc.scalar.dma_start(out=scale_col[:], in_=x_re_scale.rearrange("a b (p j) -> (a b p) j", j=4))
-            load_bytes(0)
+            make_identity(nc, ident[:])
+            for n in bias_in:
+                nc.gpsimd.dma_start(out=bias[n][:], in_=bias_in[n].rearrange("(p t) -> p t", t=4))
             load("xi0", 2)
+            load_bytes(0)
             load("wqr", 2)
             load("wqi")
             load_bytes(1)
             load("wkr")
             load("wki")
-            for n in bias_in:
-                nc.sync.dma_start(out=bias[n][:], in_=bias_in[n].rearrange("(p t) -> p t", t=4))
             load("xi1")
 
-            make_identity(nc, ident[:])
             nc.vector.memset(warm[:], 0.0)
-            nc.scalar.activation(out=warm[:], in_=warm[:], func=ACT.Identity, bias=0.0, scale=1.0)
+            nc.scalar.activation(out=dummy[:], in_=warm[:, 0:1], func=ACT.Identity, bias=0.0, scale=1.0)
+
+            bank = bank_tile()
+            for i in range(4):
+                nc.tensor.matmul(bank[:], lhsT=warm[:, 0:128], rhs=warm[:], start=True, stop=True)
 
             bank = bank_tile()
             for j in range(4):
                 nc.tensor.transpose(bank[:, 128 * j : 128 * (j + 1)], scale_col[:, j : j + 1].to_broadcast([P, P]), ident[:])
             nc.scalar.copy(out=scale_row[:].rearrange("p (n j) -> p n j", j=4), in_=bank[:].rearrange("p (j n) -> p n j", j=4))
 
-            turn("xi0")
+            turn("xi0", (0,))
             for s in range(4):
                 widen(0, s)
             turn("wqr")

@@ -34,7 +34,6 @@ def tile_teleportationattention_pa_kernel(
             return psum.tile([P, 512], F32, name="bank")
 
         ident = new("ident", [P, P], F32)
-        warm = new("warm", [P, 512], BF16)
         dummy = new("dummy", [P, 1], F32)
         scale_col = new("scale_col", [P, 4], F32)
         scale_row = new("scale_row", [P, K], F32)
@@ -171,8 +170,6 @@ def tile_teleportationattention_pa_kernel(
         with tc.manual_schedule():
             nc.scalar.dma_start(out=scale_col[:], in_=x_re_scale.rearrange("a b (p j) -> (a b p) j", j=4))
             make_identity(nc, ident[:])
-            for n in bias_in:
-                nc.gpsimd.dma_start(out=bias[n][:], in_=bias_in[n].rearrange("(p t) -> p t", t=4))
             load("xi0", 2)
             load_bytes(0)
             load("wqr", 2)
@@ -181,67 +178,63 @@ def tile_teleportationattention_pa_kernel(
             load("wkr")
             load("wki")
             load("xi1")
+            for n in bias_in:
+                nc.sync.dma_start(out=bias[n][:], in_=bias_in[n].rearrange("(p t) -> p t", t=4))
 
-            nc.vector.memset(warm[:], 0.0)
-            nc.scalar.activation(out=dummy[:], in_=warm[:, 0:1], func=ACT.Identity, bias=0.0, scale=1.0)
-
-            bank = bank_tile()
-            for i in range(4):
-                nc.tensor.matmul(bank[:], lhsT=warm[:, 0:128], rhs=warm[:], start=True, stop=True)
+            nc.vector.memset(dummy[:], 0.0)
+            nc.scalar.activation(out=dummy[:], in_=dummy[:], func=ACT.Identity, bias=0.0, scale=1.0)
 
             bank = bank_tile()
             for j in range(4):
                 nc.tensor.transpose(bank[:, 128 * j : 128 * (j + 1)], scale_col[:, j : j + 1].to_broadcast([P, P]), ident[:])
             nc.scalar.copy(out=scale_row[:].rearrange("p (n j) -> p n j", j=4), in_=bank[:].rearrange("p (j n) -> p n j", j=4))
 
-            turn("xi0", (0,))
+            turn("xi0")
             for s in range(4):
                 widen(0, s)
             turn("wqr")
-            negate(0)
-            quant("xi0")
-            turn("xr0")
             widen(1, 0)
             widen(1, 1)
-            quant("wqr")
+            negate(0)
+            turn("xr0")
             quant("xr0")
-            turn("wqi")
+            quant("xi0")
             widen(1, 2)
             widen(1, 3)
-            turn("wkr")
-            turn("wki")
-            quant("wqi")
-            quant("wkr")
-            quant("wki")
-            turn("xr1")
-            turn("xi1")
-            quant("xr1")
-            quant("xi1")
-            negate(1)
-            unit("q", "i", 0, (3,))
+            quant("wqr")
             quant("xn0")
-            unit("k", "i", 0)
+            turn("wqi")
+            quant("wqi")
+            turn("wkr")
+            quant("wkr")
+            turn("wki")
+            turn("xi1")
+            turn("xr1", (1,))
+            quant("wki")
+            negate(1)
+            quant("xi1")
+            quant("xr1")
+            unit("q", "i", 0)
             pack("qi0")
+            unit("k", "i", 0, (2,))
             pack("ki0")
-            unit("q", "i", 1, (3,))
-            quant("xn1")
-            unit("k", "i", 1)
-            pack("qi1")
             unit("q", "r", 0)
-            pack("ki1")
-            unit("k", "r", 0)
             pack("qr0")
-            unit("q", "r", 1)
+            unit("k", "r", 0)
             pack("kr0")
-            unit("k", "r", 1)
+            quant("xn1")
+            unit("q", "i", 1, (3,))
+            pack("qi1")
+            unit("k", "i", 1)
+            pack("ki1")
+            unit("q", "r", 1)
             pack("qr1")
-            banks = {}
-            for b in range(BATCHES):
-                for s in range(4):
-                    banks[b, s] = bank_tile()
-                    score_pass(banks[b, s], b, s, "i", True, False)
+            unit("k", "r", 1)
             pack("kr1")
             for b in range(BATCHES):
+                banks = [bank_tile() for s in range(4)]
                 for s in range(4):
-                    score_pass(banks[b, s], b, s, "r", False, True)
-                    score_out(banks[b, s], b, s, "vector" if (b, s) in ((0, 2), (1, 1), (1, 3)) else "scalar")
+                    score_pass(banks[s], b, s, "i", True, False)
+                for s in range(4):
+                    score_pass(banks[s], b, s, "r", False, True)
+                    score_out(banks[s], b, s, "vector" if (b, s) in ((0, 3), (1, 1), (1, 3)) else "scalar")

@@ -168,7 +168,7 @@ def tile_teleportationattention_pa_kernel(
             nc.sync.dma_start(out=out[b].rearrange("(m s) k -> m s k", s=4)[:, s, :], in_=result[b][:, s, :])
 
         with tc.manual_schedule():
-            nc.scalar.dma_start(out=scale_col[:], in_=x_re_scale.rearrange("a b (p j) -> (a b p) j", j=4))
+            nc.sync.dma_start(out=scale_col[:], in_=x_re_scale.rearrange("a b (p j) -> (a b p) j", j=4))
             make_identity(nc, ident[:])
             load("xi0", 2)
             load_bytes(0)
@@ -189,52 +189,41 @@ def tile_teleportationattention_pa_kernel(
                 nc.tensor.transpose(bank[:, 128 * j : 128 * (j + 1)], scale_col[:, j : j + 1].to_broadcast([P, P]), ident[:])
             nc.scalar.copy(out=scale_row[:].rearrange("p (n j) -> p n j", j=4), in_=bank[:].rearrange("p (j n) -> p n j", j=4))
 
-            turn("xi0")
-            for s in range(4):
-                widen(0, s)
-            turn("wqr")
-            widen(1, 0)
-            widen(1, 1)
-            negate(0)
-            turn("xr0")
-            quant("xr0")
-            quant("xi0")
-            widen(1, 2)
-            widen(1, 3)
-            quant("wqr")
-            quant("xn0")
-            turn("wqi")
-            quant("wqi")
-            turn("wkr")
-            quant("wkr")
-            turn("wki")
+            for b in range(BATCHES):
+                for s in range(4):
+                    widen(b, s)
+            for n in ("xi0", "wqr", "xr0", "wqi", "wkr", "wki"):
+                turn(n)
+                quant(n)
             turn("xi1")
-            turn("xr1", (1,))
-            quant("wki")
+            negate(0)
             negate(1)
+            quant("xn0")
             quant("xi1")
+            turn("xr1", (1,))
             quant("xr1")
             unit("q", "i", 0)
             pack("qi0")
-            unit("k", "i", 0, (2,))
+            unit("k", "i", 0)
             pack("ki0")
             unit("q", "r", 0)
             pack("qr0")
+            quant("xn1")
             unit("k", "r", 0)
             pack("kr0")
-            quant("xn1")
-            unit("q", "i", 1, (3,))
+            unit("q", "i", 1)
             pack("qi1")
             unit("k", "i", 1)
             pack("ki1")
-            unit("q", "r", 1)
-            pack("qr1")
             unit("k", "r", 1)
             pack("kr1")
-            for b in range(BATCHES):
-                banks = [bank_tile() for s in range(4)]
-                for s in range(4):
-                    score_pass(banks[s], b, s, "i", True, False)
-                for s in range(4):
-                    score_pass(banks[s], b, s, "r", False, True)
-                    score_out(banks[s], b, s, "vector" if (b, s) in ((0, 3), (1, 1), (1, 3)) else "scalar")
+            unit("q", "r", 1)
+            pack("qr1")
+            for b, group in ((0, 1), (1, 2)):
+                for first in range(0, 4, group):
+                    banks = {s: bank_tile() for s in range(first, first + group)}
+                    for s in banks:
+                        score_pass(banks[s], b, s, "i", True, False)
+                    for s in banks:
+                        score_pass(banks[s], b, s, "r", False, True)
+                        score_out(banks[s], b, s, "vector" if b == 1 and s % 2 == 1 else "scalar")

from contextlib import ExitStack

import concourse.mybir as mybir
from concourse.masks import make_identity

FLOPS = 8 * 2 * 1024 * 512 * 512 + 2 * 2 * 2 * 512 * 512 * 512

F32 = mybir.dt.float32
BF16 = mybir.dt.bfloat16
U32 = mybir.dt.uint32
U8 = mybir.dt.uint8
FP8 = mybir.dt.float8_e4m3fn
FP8X4 = mybir.dt.float8_e4m3fn_x4
ALU = mybir.AluOpType
ACT = mybir.ActivationFunctionType

P = 128
K = 512
BATCHES = 2


def tile_teleportationattention_pa_kernel(
    tc, x_re_bytes, x_re_scale, x_im, Wq_re, Wq_im, bq_re, bq_im, Wk_re, Wk_im, bk_re, bk_im, out
):
    nc = tc.nc
    with ExitStack() as ctx:
        keep = ctx.enter_context(tc.tile_pool(name="keep", bufs=1))
        psum = ctx.enter_context(tc.psum_pool(name="psum", bufs=8))

        def new(name, shape, dtype):
            return keep.tile(shape, dtype, name=name, align_bytes=64)

        def bank_tile():
            return psum.tile([P, 512], F32, name="bank")

        ident = new("ident", [P, P], F32)
        dummy = new("dummy", [P, 1], F32)
        scale_col = new("scale_col", [P, 4], F32)
        scale_row = new("scale_row", [P, K], F32)
        bias_in = {"qr": bq_re, "qi": bq_im, "kr": bk_re, "ki": bk_im}
        bias = {}
        for n in bias_in:
            bias[n] = new("bias_" + n, [P, 4], BF16)

        raw = {}
        for n in ("wqr", "wqi", "wkr", "wki", "xr0", "xi0", "xr1", "xi1"):
            raw[n] = new("raw_" + n, [P, 4, K], BF16)
        xbytes = [new("xbytes%d" % b, [P, 4, K], U8) for b in range(BATCHES)]
        grouped = {}
        codes = {}
        scales = {}
        for n in ("wqr", "wqi", "wkr", "wki", "xr0", "xi0", "xn0", "xr1", "xi1", "xn1", "qr0", "qi0", "kr0", "ki0", "qr1", "qi1", "kr1", "ki1"):
            grouped[n] = new("grp_" + n, [P, 4 * 512], BF16)
            codes[n] = new("codes_" + n, [P, 512], U32)
            scales[n] = new("scales_" + n, [P, 512], U8)
        planes = {}
        for n in ("qr0", "qi0", "kr0", "ki0", "qr1", "qi1", "kr1", "ki1"):
            planes[n] = new("planes_" + n, [P, 4, 512], BF16)
        result = [new("result%d" % b, [P, 4, 512], F32) for b in range(BATCHES)]

        w_view = {"wqr": Wq_re, "wqi": Wq_im, "wkr": Wk_re, "wki": Wk_im}
        src = {}
        for n in w_view:
            src[n] = w_view[n].rearrange("(m s) k -> m s k", s=4)
        for b in range(BATCHES):
            src["xi%d" % b] = x_im[b].rearrange("(m s) k -> m s k", s=4)

        def load(n, parts=1):
            step = 4 // parts
            for i in range(parts):
                nc.sync.dma_start(out=raw[n][:, i * step : (i + 1) * step, :], in_=src[n][:, i * step : (i + 1) * step, :])

        def load_bytes(b):
            nc.sync.dma_start(out=xbytes[b][:], in_=x_re_bytes[b].rearrange("(m s) k -> m s k", s=4))

        def widen(b, s):
            nc.vector.tensor_tensor(
                out=raw["xr%d" % b][:, s, :], in0=xbytes[b][:, s, :].bitcast(FP8), in1=scale_row[:], op=ALU.mult
            )

        def turn(n, on_vector=()):
            for h in range(2):
                bank = bank_tile()
                v = bank[:].rearrange("p (c u r) -> p c u r", c=2, u=2)
                for c in range(2):
                    words = raw[n][:, 2 * h + c, :].bitcast(F32)
                    for u in range(2):
                        nc.tensor.transpose(v[:, c, u, :], words[:, u:256:2], ident[:])
                target = grouped[n][:, 1024 * h : 1024 * (h + 1)].bitcast(F32).rearrange("p (c r u) -> p c r u", c=2, u=2)
                if h in on_vector:
                    nc.vector.tensor_copy(out=target, in_=v.rearrange("p c u r -> p c r u"))
                else:
                    nc.scalar.copy(out=target, in_=v.rearrange("p c u r -> p c r u"))

        def quant(n, h=None):
            lo, hi = (0, 512) if h is None else (256 * h, 256 * (h + 1))
            nc.vector.quantize_mx(
                out=codes[n][:, lo:hi].bitcast(FP8X4), scales=scales[n][:, lo:hi], in_=grouped[n][:, 4 * lo : 4 * hi]
            )

        def negate(b):
            nc.vector.tensor_scalar(out=grouped["xn%d" % b][:], in0=grouped["xi%d" % b][:], scalar1=-1.0, scalar2=None, op0=ALU.mult)

        def mm(bank, w, t, x, start, stop):
            nc.tensor.matmul_mx(
                out=bank[:],
                lhsT=codes[w][:, 128 * t : 128 * (t + 1)].bitcast(FP8X4),
                lhsT_scale=scales[w][:, 128 * t : 128 * (t + 1)],
                rhs=codes[x][:].bitcast(FP8X4),
                rhs_scale=scales[x][:],
                start=start,
                stop=stop,
            )

        def operands(side, part, b):
            if part == "r":
                return [("w%sr" % side, "xr%d" % b), ("w%si" % side, "xn%d" % b)]
            return [("w%sr" % side, "xi%d" % b), ("w%si" % side, "xr%d" % b)]

        def leave(bank, side, part, b, t, engine):
            plane = planes["%s%s%d" % (side, part, b)][:, t, :]
            column = bias[side + part][:, t : t + 1]
            if engine == "scalar":
                nc.scalar.activation(out=plane, in_=bank[:], func=ACT.Identity, bias=column, scale=1.0)
            else:
                nc.vector.tensor_scalar(out=plane, in0=bank[:], scalar1=column, scalar2=None, op0=ALU.add)

        def unit(side, part, b, on_vector=()):
            ops = operands(side, part, b)
            for t in range(4):
                bank = bank_tile()
                for i in range(2):
                    mm(bank, ops[i][0], t, ops[i][1], i == 0, i == 1)
                leave(bank, side, part, b, t, "vector" if t in on_vector else "scalar")

        def interleave(n, h):
            nc.vector.tensor_copy(
                out=grouped[n][:, 1024 * h : 1024 * (h + 1)].rearrange("p (c i t) -> p c t i", i=4, t=4),
                in_=planes[n][:, :, 256 * h : 256 * (h + 1)].rearrange("p t (c i) -> p c t i", i=4),
            )

        def pack(n):
            interleave(n, 0)
            interleave(n, 1)
            quant(n, 0)
            quant(n, 1)

        def score_pass(bank, b, s, part, start, stop):
            q = "q%s%d" % (part, b)
            k = "k%s%d" % (part, b)
            nc.tensor.matmul_mx(
                out=bank[:],
                lhsT=codes[q][:, 128 * s : 128 * (s + 1)].bitcast(FP8X4),
                lhsT_scale=scales[q][:, 128 * s : 128 * (s + 1)],
                rhs=codes[k][:].bitcast(FP8X4),
                rhs_scale=scales[k][:],
                start=start,
                stop=stop,
            )

        def score_out(bank, b, s, engine):
            o = result[b][:, s, :].rearrange("p (m j) -> p m j", j=4)
            i = bank[:].rearrange("p (j m) -> p m j", j=4)
            if engine == "scalar":
                nc.scalar.copy(out=o, in_=i)
            else:
                nc.vector.tensor_copy(out=o, in_=i)
            nc.sync.dma_start(out=out[b].rearrange("(m s) k -> m s k", s=4)[:, s, :], in_=result[b][:, s, :])

        with tc.manual_schedule():
            nc.sync.dma_start(out=scale_col[:], in_=x_re_scale.rearrange("a b (p j) -> (a b p) j", j=4))
            make_identity(nc, ident[:])
            load("xi0", 2)
            load_bytes(0)
            load("wqr", 2)
            load("wqi")
            load_bytes(1)
            load("wkr")
            load("wki")
            load("xi1")
            for n in bias_in:
                nc.sync.dma_start(out=bias[n][:], in_=bias_in[n].rearrange("(p t) -> p t", t=4))

            nc.vector.memset(dummy[:], 0.0)
            nc.scalar.activation(out=dummy[:], in_=dummy[:], func=ACT.Identity, bias=0.0, scale=1.0)

            bank = bank_tile()
            for j in range(4):
                nc.tensor.transpose(bank[:, 128 * j : 128 * (j + 1)], scale_col[:, j : j + 1].to_broadcast([P, P]), ident[:])
            nc.scalar.copy(out=scale_row[:].rearrange("p (n j) -> p n j", j=4), in_=bank[:].rearrange("p (j n) -> p n j", j=4))

            for b in range(BATCHES):
                for s in range(4):
                    widen(b, s)
            for n in ("xi0", "wqr", "xr0", "wqi", "wkr", "wki"):
                turn(n)
                quant(n)
            turn("xi1")
            negate(0)
            negate(1)
            quant("xn0")
            quant("xi1")
            turn("xr1", (1,))
            quant("xr1")
            unit("q", "i", 0)
            pack("qi0")
            unit("k", "i", 0)
            pack("ki0")
            unit("q", "r", 0)
            pack("qr0")
            quant("xn1")
            unit("k", "r", 0)
            pack("kr0")
            unit("q", "i", 1)
            pack("qi1")
            unit("k", "i", 1)
            pack("ki1")
            unit("k", "r", 1)
            pack("kr1")
            unit("q", "r", 1)
            pack("qr1")
            for b, group in ((0, 1), (1, 2)):
                for first in range(0, 4, group):
                    banks = {s: bank_tile() for s in range(first, first + group)}
                    for s in banks:
                        score_pass(banks[s], b, s, "i", True, False)
                    for s in banks:
                        score_pass(banks[s], b, s, "r", False, True)
                        score_out(banks[s], b, s, "vector" if b == 1 and s % 2 == 1 else "scalar")
